import numpy as np
import ml_dtypes


def mxq(x, axis, fmt="e4m3"):
    dtype, down = {"e4m3": (ml_dtypes.float8_e4m3fn, 7), "e5m2": (ml_dtypes.float8_e5m2, 14)}[fmt]
    v = np.moveaxis(np.asarray(x, np.float32).astype(ml_dtypes.bfloat16).astype(np.float64), axis, -1)
    blocks = v.reshape(v.shape[:-1] + (-1, 32))
    amax = np.abs(blocks).max(-1, keepdims=True)
    byte = np.maximum(np.where(amax > 0, np.frexp(amax)[1] - 1 + 127, 0) - down, 1)
    scale = np.exp2(byte - 127.0)
    codes = (blocks / scale).astype(np.float32).astype(dtype).astype(np.float64)
    return np.moveaxis((codes * scale).reshape(v.shape), -1, axis)


WIDE = False


def mx_kscale(k):
    if not WIDE:
        return np.ones(k)
    levels = np.array([20, -20, 10, -10, 0])
    a = np.random.permutation(np.resize(levels, k // 512 * 4)).reshape(k // 512, 4)
    idx = np.arange(k)
    return np.exp2(a[idx // 512, idx % 128 // 32])


BF16 = ml_dtypes.bfloat16


def bf(x):
    return np.asarray(x, np.float32).astype(BF16)


def f64(x):
    return np.asarray(x).astype(np.float64)


B, N, C = 1, 2048, 512
Q = N ** 0.25


def setup_inputs():
    s = mx_kscale(B * N).reshape(B, N, 1)
    msg = bf((1.4 * np.random.standard_normal((B, 1, C)) + 1.2 * np.random.standard_normal((B, N, C))) / Q)
    A = bf(np.random.uniform(0.0, 1.0, (B, N, N)) * 2.0 / N ** 0.75)
    h0 = bf(np.maximum(np.random.standard_normal((B, N, C)) * 1.35, 0.0))
    Ws = bf(np.random.uniform(-1.0, 1.0, (C, C)) * 1.5 / np.sqrt(C))
    b = bf(np.random.uniform(-1.0, 1.0, C) * 0.5)
    g = bf(np.random.standard_normal((B, N, C)) * np.exp2(np.random.randint(-12, 1, (B, N, 1))) / s)
    z = f64(A) @ f64(msg) + f64(h0) @ f64(Ws).T + f64(b)
    return {"A": A, "msg": msg, "h": bf(f64(h0) * s), "Ws": Ws, "b": b,
            "z": np.asarray(z, np.float32), "grad_out": g}


def reference(A, msg, h, Ws, b, z, grad_out):
    dz = f64(grad_out) * (f64(z) > 0.0)
    dz2 = dz.reshape(B * N, C)
    h2 = f64(h).reshape(B * N, C)
    return mxq(dz2, 0, "e5m2").T @ mxq(h2, 0, "e4m3")

@@ -1,0 +1,90 @@
+import concourse.mybir as mybir
+
+BF16 = mybir.dt.bfloat16
+F32 = mybir.dt.float32
+U32 = mybir.dt.uint32
+U8 = mybir.dt.uint8
+E4M3_X4 = mybir.dt.float8_e4m3fn_x4
+E5M2_X4 = mybir.dt.float8_e5m2_x4
+ALU = mybir.AluOpType
+
+NODES = 2048
+CH = 512
+P = 128
+PACK = 4
+K_PASS = P * PACK
+PASSES = NODES // K_PASS
+O_TILES = CH // P
+
+FLOPS = 2 * NODES * CH * CH
+BYTES = NODES * CH * (2 + 2 + 4) + CH * CH * 4
+
+
+def tile_gcnstacking_pb_v_kernel(tc, A, msg, h, Ws, b, z, grad_out, out):
+    nc = tc.nc
+    by_pass = "(c p j) w -> c p j w"
+    h_dram = h[0, :, :].rearrange(by_pass, p=P, j=PACK)
+    g_dram = grad_out[0, :, :].rearrange(by_pass, p=P, j=PACK)
+    z_dram = z[0, :, :].rearrange(by_pass, p=P, j=PACK)
+
+    with (
+        tc.tile_pool(name="loads", bufs=PASSES) as loads,
+        tc.tile_pool(name="grouped", bufs=2) as grouped,
+        tc.tile_pool(name="keep", bufs=1) as keep,
+        tc.tile_pool(name="results", bufs=O_TILES) as results,
+        tc.psum_pool(name="psum", bufs=1) as psum,
+    ):
+        h_codes = keep.tile([P, PASSES, CH], U32, align_bytes=64)
+        h_scales = keep.tile([P, PASSES, CH], U8, align_bytes=64)
+        dz_codes = keep.tile([P, PASSES, CH], U32, align_bytes=64)
+        dz_scales = keep.tile([P, PASSES, CH], U8, align_bytes=64)
+        acc = [psum.tile([P, CH], F32, name="acc%d" % o) for o in range(O_TILES)]
+
+        for c in range(PASSES):
+            h_raw = loads.tile([P, PACK, CH], BF16)
+            g_raw = loads.tile([P, PACK, CH], BF16)
+            z_raw = loads.tile([P, PACK, CH], F32)
+            nc.sync.dma_start(out=h_raw[:], in_=h_dram[c, :, :, :])
+            nc.sync.dma_start(out=g_raw[:], in_=g_dram[c, :, :, :])
+            nc.sync.dma_start(out=z_raw[:], in_=z_dram[c, :, :, :])
+
+            h_grouped = grouped.tile([P, CH, PACK], BF16, align_bytes=64)
+            nc.scalar.copy(out=h_grouped[:], in_=h_raw[:].rearrange("p j w -> p w j"))
+            dz_grouped = grouped.tile([P, CH, PACK], BF16, align_bytes=64)
+            nc.vector.scalar_tensor_tensor(
+                out=dz_grouped[:],
+                in0=z_raw[:].rearrange("p j w -> p w j"),
+                scalar=0.0,
+                in1=g_raw[:].rearrange("p j w -> p w j"),
+                op0=ALU.is_gt,
+                op1=ALU.mult,
+            )
+            nc.vector.quantize_mx(
+                out=h_codes[:, c, :].bitcast(E4M3_X4),
+                scales=h_scales[:, c, :],
+                in_=h_grouped[:].rearrange("p w j -> p (w j)"),
+            )
+            nc.vector.quantize_mx(
+                out=dz_codes[:, c, :].bitcast(E5M2_X4),
+                scales=dz_scales[:, c, :],
+                in_=dz_grouped[:].rearrange("p w j -> p (w j)"),
+            )
+            for o in range(O_TILES):
+                o_cols = slice(o * P, (o + 1) * P)
+                nc.tensor.matmul_mx(
+                    out=acc[o][:],
+                    lhsT=dz_codes[:, c, o_cols].bitcast(E5M2_X4),
+                    lhsT_scale=dz_scales[:, c, o_cols],
+                    rhs=h_codes[:, c, :].bitcast(E4M3_X4),
+                    rhs_scale=h_scales[:, c, :],
+                    start=(c == 0),
+                    stop=(c == PASSES - 1),
+                )
+
+        for o in range(O_TILES):
+            result = results.tile([P, CH], F32)
+            if o % 2 == 0:
+                nc.scalar.copy(out=result[:], in_=acc[o][:])
+            else:
+                nc.vector.tensor_copy(out=result[:], in_=acc[o][:])
+            nc.sync.dma_start(out=out[o * P : (o + 1) * P, :], in_=result[:])

@@ -29,7 +29,7 @@ def tile_gcnstacking_pb_v_kernel(tc, A, msg, h, Ws, b, z, grad_out, out):
 
     with (
         tc.tile_pool(name="loads", bufs=PASSES) as loads,
-        tc.tile_pool(name="grouped", bufs=2) as grouped,
+        tc.tile_pool(name="grouped", bufs=O_TILES) as grouped,
         tc.tile_pool(name="keep", bufs=1) as keep,
         tc.tile_pool(name="results", bufs=O_TILES) as results,
         tc.psum_pool(name="psum", bufs=1) as psum,
@@ -40,36 +40,42 @@ def tile_gcnstacking_pb_v_kernel(tc, A, msg, h, Ws, b, z, grad_out, out):
         dz_scales = keep.tile([P, PASSES, CH], U8, align_bytes=64)
         acc = [psum.tile([P, CH], F32, name="acc%d" % o) for o in range(O_TILES)]
 
-        for c in range(PASSES):
+        def fetch_h(c):
             h_raw = loads.tile([P, PACK, CH], BF16)
-            g_raw = loads.tile([P, PACK, CH], BF16)
-            z_raw = loads.tile([P, PACK, CH], F32)
             nc.sync.dma_start(out=h_raw[:], in_=h_dram[c, :, :, :])
-            nc.sync.dma_start(out=g_raw[:], in_=g_dram[c, :, :, :])
-            nc.sync.dma_start(out=z_raw[:], in_=z_dram[c, :, :, :])
-
             h_grouped = grouped.tile([P, CH, PACK], BF16, align_bytes=64)
             nc.scalar.copy(out=h_grouped[:], in_=h_raw[:].rearrange("p j w -> p w j"))
-            dz_grouped = grouped.tile([P, CH, PACK], BF16, align_bytes=64)
-            nc.vector.scalar_tensor_tensor(
-                out=dz_grouped[:],
-                in0=z_raw[:].rearrange("p j w -> p w j"),
-                scalar=0.0,
-                in1=g_raw[:].rearrange("p j w -> p w j"),
-                op0=ALU.is_gt,
-                op1=ALU.mult,
-            )
+            return h_grouped
+
+        def quantise_h(c, h_grouped):
             nc.vector.quantize_mx(
                 out=h_codes[:, c, :].bitcast(E4M3_X4),
                 scales=h_scales[:, c, :],
                 in_=h_grouped[:].rearrange("p w j -> p (w j)"),
             )
+
+        def mask(z_raw, g_raw, lo, width):
+            dz_grouped = grouped.tile(
+                [P, width, PACK], BF16, tag="dz_grouped%d" % width, align_bytes=64
+            )
+            nc.vector.scalar_tensor_tensor(
+                out=dz_grouped[:],
+                in0=z_raw[:].rearrange("p j w -> p w j"),
+                scalar=0.0,
+                in1=g_raw[:, :, lo : lo + width].rearrange("p j w -> p w j"),
+                op0=ALU.is_gt,
+                op1=ALU.mult,
+            )
+            return dz_grouped
+
+        def multiply(c, dz_grouped, lo, width):
+            cols = slice(lo, lo + width)
             nc.vector.quantize_mx(
-                out=dz_codes[:, c, :].bitcast(E5M2_X4),
-                scales=dz_scales[:, c, :],
+                out=dz_codes[:, c, cols].bitcast(E5M2_X4),
+                scales=dz_scales[:, c, cols],
                 in_=dz_grouped[:].rearrange("p w j -> p (w j)"),
             )
-            for o in range(O_TILES):
+            for o in range(lo // P, (lo + width) // P):
                 o_cols = slice(o * P, (o + 1) * P)
                 nc.tensor.matmul_mx(
                     out=acc[o][:],
@@ -80,11 +86,31 @@ def tile_gcnstacking_pb_v_kernel(tc, A, msg, h, Ws, b, z, grad_out, out):
                     start=(c == 0),
                     stop=(c == PASSES - 1),
                 )
+                if c == PASSES - 1:
+                    result = results.tile([P, CH], F32)
+                    nc.scalar.copy(out=result[:], in_=acc[o][:])
+                    nc.sync.dma_start(out=out[o_cols, :], in_=result[:])
 
-        for o in range(O_TILES):
-            result = results.tile([P, CH], F32)
-            if o % 2 == 0:
-                nc.scalar.copy(out=result[:], in_=acc[o][:])
-            else:
-                nc.vector.tensor_copy(out=result[:], in_=acc[o][:])
-            nc.sync.dma_start(out=out[o * P : (o + 1) * P, :], in_=result[:])
+        quantise_h(0, fetch_h(0))
+        for c in range(PASSES):
+            last = c == PASSES - 1
+            if not last:
+                h_next = fetch_h(c + 1)
+            g_raw = loads.tile([P, PACK, CH], BF16)
+            nc.sync.dma_start(out=g_raw[:], in_=g_dram[c, :, :, :])
+
+            width = P if last else CH
+            z_raws = []
+            for lo in range(0, CH, width):
+                z_raw = loads.tile([P, PACK, width], F32, tag="z_raw%d" % width)
+                nc.sync.dma_start(out=z_raw[:], in_=z_dram[c, :, :, lo : lo + width])
+                z_raws.append(z_raw)
+
+            for s, z_raw in enumerate(z_raws):
+                dz_grouped = mask(z_raw, g_raw, s * width, width)
+                if s > 0:
+                    multiply(c, dz_before, (s - 1) * width, width)
+                elif not last:
+                    quantise_h(c + 1, h_next)
+                dz_before = dz_grouped
+            multiply(c, dz_before, CH - width, width)

@@ -91,11 +91,9 @@ def tile_gcnstacking_pb_v_kernel(tc, A, msg, h, Ws, b, z, grad_out, out):
                     nc.scalar.copy(out=result[:], in_=acc[o][:])
                     nc.sync.dma_start(out=out[o_cols, :], in_=result[:])
 
-        quantise_h(0, fetch_h(0))
         for c in range(PASSES):
             last = c == PASSES - 1
-            if not last:
-                h_next = fetch_h(c + 1)
+            h_grouped = fetch_h(c)
             g_raw = loads.tile([P, PACK, CH], BF16)
             nc.sync.dma_start(out=g_raw[:], in_=g_dram[c, :, :, :])
 
@@ -108,9 +106,9 @@ def tile_gcnstacking_pb_v_kernel(tc, A, msg, h, Ws, b, z, grad_out, out):
 
             for s, z_raw in enumerate(z_raws):
                 dz_grouped = mask(z_raw, g_raw, s * width, width)
-                if s > 0:
+                if s == 0:
+                    quantise_h(c, h_grouped)
+                else:
                     multiply(c, dz_before, (s - 1) * width, width)
-                elif not last:
-                    quantise_h(c + 1, h_next)
                 dz_before = dz_grouped
             multiply(c, dz_before, CH - width, width)

@@ -26,13 +26,16 @@ def tile_gcnstacking_pb_v_kernel(tc, A, msg, h, Ws, b, z, grad_out, out):
     h_dram = h[0, :, :].rearrange(by_pass, p=P, j=PACK)
     g_dram = grad_out[0, :, :].rearrange(by_pass, p=P, j=PACK)
     z_dram = z[0, :, :].rearrange(by_pass, p=P, j=PACK)
+    LAST = PASSES - 1
+    HALF = CH // 2
 
     with (
         tc.tile_pool(name="loads", bufs=PASSES) as loads,
-        tc.tile_pool(name="grouped", bufs=O_TILES) as grouped,
+        tc.tile_pool(name="grouped", bufs=PASSES) as grouped,
         tc.tile_pool(name="keep", bufs=1) as keep,
         tc.tile_pool(name="results", bufs=O_TILES) as results,
         tc.psum_pool(name="psum", bufs=1) as psum,
+        tc.manual_schedule(),
     ):
         h_codes = keep.tile([P, PASSES, CH], U32, align_bytes=64)
         h_scales = keep.tile([P, PASSES, CH], U8, align_bytes=64)
@@ -40,40 +43,49 @@ def tile_gcnstacking_pb_v_kernel(tc, A, msg, h, Ws, b, z, grad_out, out):
         dz_scales = keep.tile([P, PASSES, CH], U8, align_bytes=64)
         acc = [psum.tile([P, CH], F32, name="acc%d" % o) for o in range(O_TILES)]
 
-        def fetch_h(c):
-            h_raw = loads.tile([P, PACK, CH], BF16)
-            nc.sync.dma_start(out=h_raw[:], in_=h_dram[c, :, :, :])
-            h_grouped = grouped.tile([P, CH, PACK], BF16, align_bytes=64)
-            nc.scalar.copy(out=h_grouped[:], in_=h_raw[:].rearrange("p j w -> p w j"))
-            return h_grouped
+        h_raw, g_raw, z_raw = [], [], []
+        for c in range(PASSES):
+            h_tile = loads.tile([P, PACK, CH], BF16, tag="h_raw")
+            nc.sync.dma_start(out=h_tile[:], in_=h_dram[c, :, :, :])
+            h_raw.append(h_tile)
+            g_tile = loads.tile([P, PACK, CH], BF16, tag="g_raw")
+            nc.sync.dma_start(out=g_tile[:], in_=g_dram[c, :, :, :])
+            g_raw.append(g_tile)
+            z_tile = loads.tile([P, PACK, CH], F32, tag="z_raw")
+            width = P if c == LAST else CH
+            for lo in range(0, CH, width):
+                nc.sync.dma_start(out=z_tile[:, :, lo : lo + width], in_=z_dram[c, :, :, lo : lo + width])
+            z_raw.append(z_tile)
 
-        def quantise_h(c, h_grouped):
+        h_grouped = [grouped.tile([P, CH, PACK], BF16, tag="h_grouped", name="h_grouped%d" % c, align_bytes=64) for c in range(PASSES)]
+        dz_grouped = [grouped.tile([P, CH, PACK], BF16, tag="dz_grouped", name="dz_grouped%d" % c, align_bytes=64) for c in range(PASSES)]
+
+        def interleave_h(c):
+            nc.scalar.copy(out=h_grouped[c][:], in_=h_raw[c][:].rearrange("p j w -> p w j"))
+
+        def quantise_h(c):
             nc.vector.quantize_mx(
                 out=h_codes[:, c, :].bitcast(E4M3_X4),
                 scales=h_scales[:, c, :],
-                in_=h_grouped[:].rearrange("p w j -> p (w j)"),
+                in_=h_grouped[c][:].rearrange("p w j -> p (w j)"),
             )
 
-        def mask(z_raw, g_raw, lo, width):
-            dz_grouped = grouped.tile(
-                [P, width, PACK], BF16, tag="dz_grouped%d" % width, align_bytes=64
-            )
+        def mask(c, lo, width):
             nc.vector.scalar_tensor_tensor(
-                out=dz_grouped[:],
-                in0=z_raw[:].rearrange("p j w -> p w j"),
+                out=dz_grouped[c][:, lo : lo + width, :],
+                in0=z_raw[c][:, :, lo : lo + width].rearrange("p j w -> p w j"),
                 scalar=0.0,
-                in1=g_raw[:, :, lo : lo + width].rearrange("p j w -> p w j"),
+                in1=g_raw[c][:, :, lo : lo + width].rearrange("p j w -> p w j"),
                 op0=ALU.is_gt,
                 op1=ALU.mult,
             )
-            return dz_grouped
 
-        def multiply(c, dz_grouped, lo, width):
+        def multiply(c, lo, width):
             cols = slice(lo, lo + width)
             nc.vector.quantize_mx(
                 out=dz_codes[:, c, cols].bitcast(E5M2_X4),
                 scales=dz_scales[:, c, cols],
-                in_=dz_grouped[:].rearrange("p w j -> p (w j)"),
+                in_=dz_grouped[c][:, cols, :].rearrange("p w j -> p (w j)"),
             )
             for o in range(lo // P, (lo + width) // P):
                 o_cols = slice(o * P, (o + 1) * P)
@@ -84,31 +96,30 @@ def tile_gcnstacking_pb_v_kernel(tc, A, msg, h, Ws, b, z, grad_out, out):
                     rhs=h_codes[:, c, :].bitcast(E4M3_X4),
                     rhs_scale=h_scales[:, c, :],
                     start=(c == 0),
-                    stop=(c == PASSES - 1),
+                    stop=(c == LAST),
                 )
-                if c == PASSES - 1:
+                if c == LAST:
                     result = results.tile([P, CH], F32)
-                    nc.scalar.copy(out=result[:], in_=acc[o][:])
+                    if o == O_TILES - 1:
+                        nc.vector.tensor_copy(out=result[:], in_=acc[o][:])
+                    else:
+                        nc.scalar.copy(out=result[:], in_=acc[o][:])
                     nc.sync.dma_start(out=out[o_cols, :], in_=result[:])
 
-        for c in range(PASSES):
-            last = c == PASSES - 1
-            h_grouped = fetch_h(c)
-            g_raw = loads.tile([P, PACK, CH], BF16)
-            nc.sync.dma_start(out=g_raw[:], in_=g_dram[c, :, :, :])
-
-            width = P if last else CH
-            z_raws = []
-            for lo in range(0, CH, width):
-                z_raw = loads.tile([P, PACK, width], F32, tag="z_raw%d" % width)
-                nc.sync.dma_start(out=z_raw[:], in_=z_dram[c, :, :, lo : lo + width])
-                z_raws.append(z_raw)
-
-            for s, z_raw in enumerate(z_raws):
-                dz_grouped = mask(z_raw, g_raw, s * width, width)
-                if s == 0:
-                    quantise_h(c, h_grouped)
-                else:
-                    multiply(c, dz_before, (s - 1) * width, width)
-                dz_before = dz_grouped
-            multiply(c, dz_before, CH - width, width)
+        for c in range(LAST):
+            interleave_h(c)
+            quantise_h(c)
+            mask(c, 0, HALF)
+            mask(c, HALF, HALF)
+            multiply(c, 0, HALF)
+            multiply(c, HALF, HALF)
+        interleave_h(LAST)
+        mask(LAST, 0, P)
+        mask(LAST, P, P)
+        quantise_h(LAST)
+        multiply(LAST, 0, P)
+        multiply(LAST, P, P)
+        mask(LAST, 2 * P, P)
+        mask(LAST, 3 * P, P)
+        multiply(LAST, 2 * P, P)
+        multiply(LAST, 3 * P, P)

@@ -42,6 +42,7 @@ def tile_gcnstacking_pb_v_kernel(tc, A, msg, h, Ws, b, z, grad_out, out):
         dz_codes = keep.tile([P, PASSES, CH], U32, align_bytes=64)
         dz_scales = keep.tile([P, PASSES, CH], U8, align_bytes=64)
         acc = [psum.tile([P, CH], F32, name="acc%d" % o) for o in range(O_TILES)]
+        idle_bank = psum.tile([P, CH], F32, name="idle_bank")
 
         h_raw, g_raw, z_raw = [], [], []
         for c in range(PASSES):
@@ -80,13 +81,23 @@ def tile_gcnstacking_pb_v_kernel(tc, A, msg, h, Ws, b, z, grad_out, out):
                 op1=ALU.mult,
             )
 
-        def multiply(c, lo, width):
+        def keep_busy(tile_view):
+            flat = tile_view.rearrange("p w j -> p (w j)")
+            nc.tensor.matmul(out=idle_bank[:], lhsT=flat[:, 0:P], rhs=flat, start=True, stop=True)
+
+        def quantise_dz(c, lo, width):
             cols = slice(lo, lo + width)
             nc.vector.quantize_mx(
                 out=dz_codes[:, c, cols].bitcast(E5M2_X4),
                 scales=dz_scales[:, c, cols],
                 in_=dz_grouped[c][:, cols, :].rearrange("p w j -> p (w j)"),
             )
+
+        def multiply(c, lo, width):
+            quantise_dz(c, lo, width)
+            passes_of(c, lo, width)
+
+        def passes_of(c, lo, width):
             for o in range(lo // P, (lo + width) // P):
                 o_cols = slice(o * P, (o + 1) * P)
                 nc.tensor.matmul_mx(
@@ -101,25 +112,39 @@ def tile_gcnstacking_pb_v_kernel(tc, A, msg, h, Ws, b, z, grad_out, out):
                 if c == LAST:
                     result = results.tile([P, CH], F32)
                     if o == O_TILES - 1:
-                        nc.vector.tensor_copy(out=result[:], in_=acc[o][:])
+                        for i_lo in (0, HALF):
+                            i_cols = slice(i_lo, i_lo + HALF)
+                            nc.vector.tensor_copy(out=result[:, i_cols], in_=acc[o][:, i_cols])
+                            nc.sync.dma_start(out=out[o_cols, i_cols], in_=result[:, i_cols])
                     else:
                         nc.scalar.copy(out=result[:], in_=acc[o][:])
-                    nc.sync.dma_start(out=out[o_cols, :], in_=result[:])
+                        nc.sync.dma_start(out=out[o_cols, :], in_=result[:])
 
         for c in range(LAST):
             interleave_h(c)
+            if c == 2:
+                keep_busy(h_grouped[c][:, 0:P, :])
+                passes_of(1, 0, CH)
             quantise_h(c)
             mask(c, 0, HALF)
             mask(c, HALF, HALF)
-            multiply(c, 0, HALF)
-            multiply(c, HALF, HALF)
+            if c == 1:
+                quantise_dz(c, 0, HALF)
+                quantise_dz(c, HALF, HALF)
+            else:
+                multiply(c, 0, HALF)
+                multiply(c, HALF, HALF)
         interleave_h(LAST)
         mask(LAST, 0, P)
+        keep_busy(dz_grouped[LAST][:, 0:P, :])
         mask(LAST, P, P)
+        keep_busy(dz_grouped[LAST][:, P : 2 * P, :])
         quantise_h(LAST)
         multiply(LAST, 0, P)
-        multiply(LAST, P, P)
         mask(LAST, 2 * P, P)
-        mask(LAST, 3 * P, P)
+        multiply(LAST, P, P)
         multiply(LAST, 2 * P, P)
-        multiply(LAST, 3 * P, P)
+        mask(LAST, 3 * P, P // 2)
+        mask(LAST, 3 * P + P // 2, P // 2)
+        quantise_dz(LAST, 3 * P, P // 2)
+        multiply(LAST, 3 * P + P // 2, P // 2)

@@ -58,6 +58,8 @@ def tile_gcnstacking_pb_v_kernel(tc, A, msg, h, Ws, b, z, grad_out, out):
                 nc.sync.dma_start(out=z_tile[:, :, lo : lo + width], in_=z_dram[c, :, :, lo : lo + width])
             z_raw.append(z_tile)
 
+        g_grouped = grouped.tile([P, CH, PACK], BF16, tag="g_grouped", align_bytes=64)
+        above_zero = grouped.tile([P, CH, PACK], BF16, tag="above_zero", align_bytes=64)
         h_grouped = [grouped.tile([P, CH, PACK], BF16, tag="h_grouped", name="h_grouped%d" % c, align_bytes=64) for c in range(PASSES)]
         dz_grouped = [grouped.tile([P, CH, PACK], BF16, tag="dz_grouped", name="dz_grouped%d" % c, align_bytes=64) for c in range(PASSES)]
 
@@ -79,6 +81,32 @@ def tile_gcnstacking_pb_v_kernel(tc, A, msg, h, Ws, b, z, grad_out, out):
                 in1=g_raw[c][:, :, lo : lo + width].rearrange("p j w -> p w j"),
                 op0=ALU.is_gt,
                 op1=ALU.mult,
+            )
+
+        def interleave_g(c, lo, width):
+            cols = slice(lo, lo + width)
+            nc.scalar.copy(
+                out=g_grouped[:, cols, :].rearrange("p (b i) j -> p b j i", i=4),
+                in_=g_raw[c][:, :, cols].rearrange("p j (b i) -> p b j i", i=4),
+            )
+
+        def compare(c, lo, width):
+            cols = slice(lo, lo + width)
+            nc.vector.tensor_scalar(
+                out=above_zero[:, cols, :].rearrange("p (b i) j -> p b j i", i=4),
+                in0=z_raw[c][:, :, cols].rearrange("p j (b i) -> p b j i", i=4),
+                scalar1=0.0,
+                scalar2=None,
+                op0=ALU.is_gt,
+            )
+
+        def select(c, lo, width):
+            cols = slice(lo, lo + width)
+            nc.vector.tensor_tensor(
+                out=dz_grouped[c][:, cols, :].rearrange("p w j -> p (w j)"),
+                in0=above_zero[:, cols, :].rearrange("p w j -> p (w j)"),
+                in1=g_grouped[:, cols, :].rearrange("p w j -> p (w j)"),
+                op=ALU.mult,
             )
 
         def keep_busy(tile_view):
@@ -126,8 +154,16 @@ def tile_gcnstacking_pb_v_kernel(tc, A, msg, h, Ws, b, z, grad_out, out):
                 keep_busy(h_grouped[c][:, 0:P, :])
                 passes_of(1, 0, CH)
             quantise_h(c)
-            mask(c, 0, HALF)
-            mask(c, HALF, HALF)
+            if c == 2:
+                interleave_g(c, 0, HALF)
+                interleave_g(c, HALF, HALF)
+                compare(c, 0, HALF)
+                compare(c, HALF, HALF)
+                select(c, 0, HALF)
+                select(c, HALF, HALF)
+            else:
+                mask(c, 0, HALF)
+                mask(c, HALF, HALF)
             if c == 1:
                 quantise_dz(c, 0, HALF)
                 quantise_dz(c, HALF, HALF)

@@ -64,7 +64,10 @@ def tile_gcnstacking_pb_v_kernel(tc, A, msg, h, Ws, b, z, grad_out, out):
         dz_grouped = [grouped.tile([P, CH, PACK], BF16, tag="dz_grouped", name="dz_grouped%d" % c, align_bytes=64) for c in range(PASSES)]
 
         def interleave_h(c):
-            nc.scalar.copy(out=h_grouped[c][:], in_=h_raw[c][:].rearrange("p j w -> p w j"))
+            nc.scalar.copy(
+                out=h_grouped[c][:].rearrange("p (b i) j -> p b j i", i=4),
+                in_=h_raw[c][:].rearrange("p j (b i) -> p b j i", i=4),
+            )
 
         def quantise_h(c):
             nc.vector.quantize_mx(
@@ -177,10 +180,10 @@ def tile_gcnstacking_pb_v_kernel(tc, A, msg, h, Ws, b, z, grad_out, out):
         keep_busy(dz_grouped[LAST][:, P : 2 * P, :])
         quantise_h(LAST)
         multiply(LAST, 0, P)
-        mask(LAST, 2 * P, P)
         multiply(LAST, P, P)
-        multiply(LAST, 2 * P, P)
+        mask(LAST, 2 * P, P)
         mask(LAST, 3 * P, P // 2)
+        multiply(LAST, 2 * P, P)
         mask(LAST, 3 * P + P // 2, P // 2)
         quantise_dz(LAST, 3 * P, P // 2)
         multiply(LAST, 3 * P + P // 2, P // 2)

@@ -50,13 +50,20 @@ def tile_gcnstacking_pb_v_kernel(tc, A, msg, h, Ws, b, z, grad_out, out):
             nc.sync.dma_start(out=h_tile[:], in_=h_dram[c, :, :, :])
             h_raw.append(h_tile)
             g_tile = loads.tile([P, PACK, CH], BF16, tag="g_raw")
-            nc.sync.dma_start(out=g_tile[:], in_=g_dram[c, :, :, :])
             g_raw.append(g_tile)
             z_tile = loads.tile([P, PACK, CH], F32, tag="z_raw")
-            width = P if c == LAST else CH
-            for lo in range(0, CH, width):
-                nc.sync.dma_start(out=z_tile[:, :, lo : lo + width], in_=z_dram[c, :, :, lo : lo + width])
             z_raw.append(z_tile)
+            if c == LAST:
+                for lo in range(0, CH, HALF):
+                    nc.sync.dma_start(out=g_tile[:, :, lo : lo + HALF], in_=g_dram[c, :, :, lo : lo + HALF])
+                    for z_lo in (lo, lo + P):
+                        nc.sync.dma_start(out=z_tile[:, :, z_lo : z_lo + P], in_=z_dram[c, :, :, z_lo : z_lo + P])
+            elif c == 2:
+                nc.sync.dma_start(out=z_tile[:], in_=z_dram[c, :, :, :])
+                nc.sync.dma_start(out=g_tile[:], in_=g_dram[c, :, :, :])
+            else:
+                nc.sync.dma_start(out=g_tile[:], in_=g_dram[c, :, :, :])
+                nc.sync.dma_start(out=z_tile[:], in_=z_dram[c, :, :, :])
 
         g_grouped = grouped.tile([P, CH, PACK], BF16, tag="g_grouped", align_bytes=64)
         above_zero = grouped.tile([P, CH, PACK], BF16, tag="above_zero", align_bytes=64)
@@ -156,16 +163,14 @@ def tile_gcnstacking_pb_v_kernel(tc, A, msg, h, Ws, b, z, grad_out, out):
             if c == 2:
                 keep_busy(h_grouped[c][:, 0:P, :])
                 passes_of(1, 0, CH)
-            quantise_h(c)
             if c == 2:
-                interleave_g(c, 0, HALF)
                 interleave_g(c, HALF, HALF)
-                compare(c, 0, HALF)
                 compare(c, HALF, HALF)
-                select(c, 0, HALF)
+            quantise_h(c)
+            mask(c, 0, HALF)
+            if c == 2:
                 select(c, HALF, HALF)
             else:
-                mask(c, 0, HALF)
                 mask(c, HALF, HALF)
             if c == 1:
                 quantise_dz(c, 0, HALF)

@@ -42,7 +42,6 @@ def tile_gcnstacking_pb_v_kernel(tc, A, msg, h, Ws, b, z, grad_out, out):
         dz_codes = keep.tile([P, PASSES, CH], U32, align_bytes=64)
         dz_scales = keep.tile([P, PASSES, CH], U8, align_bytes=64)
         acc = [psum.tile([P, CH], F32, name="acc%d" % o) for o in range(O_TILES)]
-        idle_bank = psum.tile([P, CH], F32, name="idle_bank")
 
         h_raw, g_raw, z_raw = [], [], []
         for c in range(PASSES):
@@ -58,15 +57,15 @@ def tile_gcnstacking_pb_v_kernel(tc, A, msg, h, Ws, b, z, grad_out, out):
                     nc.sync.dma_start(out=g_tile[:, :, lo : lo + HALF], in_=g_dram[c, :, :, lo : lo + HALF])
                     for z_lo in (lo, lo + P):
                         nc.sync.dma_start(out=z_tile[:, :, z_lo : z_lo + P], in_=z_dram[c, :, :, z_lo : z_lo + P])
-            elif c == 2:
+            elif c >= 1:
                 nc.sync.dma_start(out=z_tile[:], in_=z_dram[c, :, :, :])
                 nc.sync.dma_start(out=g_tile[:], in_=g_dram[c, :, :, :])
             else:
                 nc.sync.dma_start(out=g_tile[:], in_=g_dram[c, :, :, :])
                 nc.sync.dma_start(out=z_tile[:], in_=z_dram[c, :, :, :])
 
-        g_grouped = grouped.tile([P, CH, PACK], BF16, tag="g_grouped", align_bytes=64)
-        above_zero = grouped.tile([P, CH, PACK], BF16, tag="above_zero", align_bytes=64)
+        g_grouped = [grouped.tile([P, CH, PACK], BF16, tag="g_grouped", name="g_grouped%d" % c, align_bytes=64) for c in range(PASSES)]
+        above_zero = [grouped.tile([P, CH, PACK], BF16, tag="above_zero", name="above_zero%d" % c, align_bytes=64) for c in range(PASSES)]
         h_grouped = [grouped.tile([P, CH, PACK], BF16, tag="h_grouped", name="h_grouped%d" % c, align_bytes=64) for c in range(PASSES)]
         dz_grouped = [grouped.tile([P, CH, PACK], BF16, tag="dz_grouped", name="dz_grouped%d" % c, align_bytes=64) for c in range(PASSES)]
 
@@ -96,14 +95,14 @@ def tile_gcnstacking_pb_v_kernel(tc, A, msg, h, Ws, b, z, grad_out, out):
         def interleave_g(c, lo, width):
             cols = slice(lo, lo + width)
             nc.scalar.copy(
-                out=g_grouped[:, cols, :].rearrange("p (b i) j -> p b j i", i=4),
+                out=g_grouped[c][:, cols, :].rearrange("p (b i) j -> p b j i", i=4),
                 in_=g_raw[c][:, :, cols].rearrange("p j (b i) -> p b j i", i=4),
             )
 
         def compare(c, lo, width):
             cols = slice(lo, lo + width)
             nc.vector.tensor_scalar(
-                out=above_zero[:, cols, :].rearrange("p (b i) j -> p b j i", i=4),
+                out=above_zero[c][:, cols, :].rearrange("p (b i) j -> p b j i", i=4),
                 in0=z_raw[c][:, :, cols].rearrange("p j (b i) -> p b j i", i=4),
                 scalar1=0.0,
                 scalar2=None,
@@ -114,14 +113,10 @@ def tile_gcnstacking_pb_v_kernel(tc, A, msg, h, Ws, b, z, grad_out, out):
             cols = slice(lo, lo + width)
             nc.vector.tensor_tensor(
                 out=dz_grouped[c][:, cols, :].rearrange("p w j -> p (w j)"),
-                in0=above_zero[:, cols, :].rearrange("p w j -> p (w j)"),
-                in1=g_grouped[:, cols, :].rearrange("p w j -> p (w j)"),
+                in0=above_zero[c][:, cols, :].rearrange("p w j -> p (w j)"),
+                in1=g_grouped[c][:, cols, :].rearrange("p w j -> p (w j)"),
                 op=ALU.mult,
             )
-
-        def keep_busy(tile_view):
-            flat = tile_view.rearrange("p w j -> p (w j)")
-            nc.tensor.matmul(out=idle_bank[:], lhsT=flat[:, 0:P], rhs=flat, start=True, stop=True)
 
         def quantise_dz(c, lo, width):
             cols = slice(lo, lo + width)
@@ -161,14 +156,13 @@ def tile_gcnstacking_pb_v_kernel(tc, A, msg, h, Ws, b, z, grad_out, out):
         for c in range(LAST):
             interleave_h(c)
             if c == 2:
-                keep_busy(h_grouped[c][:, 0:P, :])
                 passes_of(1, 0, CH)
-            if c == 2:
+            if c >= 1:
                 interleave_g(c, HALF, HALF)
                 compare(c, HALF, HALF)
             quantise_h(c)
             mask(c, 0, HALF)
-            if c == 2:
+            if c >= 1:
                 select(c, HALF, HALF)
             else:
                 mask(c, HALF, HALF)
@@ -180,12 +174,9 @@ def tile_gcnstacking_pb_v_kernel(tc, A, msg, h, Ws, b, z, grad_out, out):
                 multiply(c, HALF, HALF)
         interleave_h(LAST)
         mask(LAST, 0, P)
-        keep_busy(dz_grouped[LAST][:, 0:P, :])
         mask(LAST, P, P)
-        keep_busy(dz_grouped[LAST][:, P : 2 * P, :])
         quantise_h(LAST)
-        multiply(LAST, 0, P)
-        multiply(LAST, P, P)
+        multiply(LAST, 0, HALF)
         mask(LAST, 2 * P, P)
         mask(LAST, 3 * P, P // 2)
         multiply(LAST, 2 * P, P)

import concourse.mybir as mybir

BF16 = mybir.dt.bfloat16
F32 = mybir.dt.float32
U32 = mybir.dt.uint32
U8 = mybir.dt.uint8
E4M3_X4 = mybir.dt.float8_e4m3fn_x4
E5M2_X4 = mybir.dt.float8_e5m2_x4
ALU = mybir.AluOpType

NODES = 2048
CH = 512
P = 128
PACK = 4
K_PASS = P * PACK
PASSES = NODES // K_PASS
O_TILES = CH // P

FLOPS = 2 * NODES * CH * CH
BYTES = NODES * CH * (2 + 2 + 4) + CH * CH * 4


def tile_gcnstacking_pb_v_kernel(tc, A, msg, h, Ws, b, z, grad_out, out):
    nc = tc.nc
    by_pass = "(c p j) w -> c p j w"
    h_dram = h[0, :, :].rearrange(by_pass, p=P, j=PACK)
    g_dram = grad_out[0, :, :].rearrange(by_pass, p=P, j=PACK)
    z_dram = z[0, :, :].rearrange(by_pass, p=P, j=PACK)
    LAST = PASSES - 1
    HALF = CH // 2

    with (
        tc.tile_pool(name="loads", bufs=PASSES) as loads,
        tc.tile_pool(name="grouped", bufs=PASSES) as grouped,
        tc.tile_pool(name="keep", bufs=1) as keep,
        tc.tile_pool(name="results", bufs=O_TILES) as results,
        tc.psum_pool(name="psum", bufs=1) as psum,
        tc.manual_schedule(),
    ):
        h_codes = keep.tile([P, PASSES, CH], U32, align_bytes=64)
        h_scales = keep.tile([P, PASSES, CH], U8, align_bytes=64)
        dz_codes = keep.tile([P, PASSES, CH], U32, align_bytes=64)
        dz_scales = keep.tile([P, PASSES, CH], U8, align_bytes=64)
        acc = [psum.tile([P, CH], F32, name="acc%d" % o) for o in range(O_TILES)]

        h_raw, g_raw, z_raw = [], [], []
        for c in range(PASSES):
            h_tile = loads.tile([P, PACK, CH], BF16, tag="h_raw")
            nc.sync.dma_start(out=h_tile[:], in_=h_dram[c, :, :, :])
            h_raw.append(h_tile)
            g_tile = loads.tile([P, PACK, CH], BF16, tag="g_raw")
            g_raw.append(g_tile)
            z_tile = loads.tile([P, PACK, CH], F32, tag="z_raw")
            z_raw.append(z_tile)
            if c == LAST:
                for lo in range(0, CH, HALF):
                    nc.sync.dma_start(out=g_tile[:, :, lo : lo + HALF], in_=g_dram[c, :, :, lo : lo + HALF])
                    for z_lo in (lo, lo + P):
                        nc.sync.dma_start(out=z_tile[:, :, z_lo : z_lo + P], in_=z_dram[c, :, :, z_lo : z_lo + P])
            elif c >= 1:
                nc.sync.dma_start(out=z_tile[:], in_=z_dram[c, :, :, :])
                nc.sync.dma_start(out=g_tile[:], in_=g_dram[c, :, :, :])
            else:
                nc.sync.dma_start(out=g_tile[:], in_=g_dram[c, :, :, :])
                nc.sync.dma_start(out=z_tile[:], in_=z_dram[c, :, :, :])

        g_grouped = [grouped.tile([P, CH, PACK], BF16, tag="g_grouped", name="g_grouped%d" % c, align_bytes=64) for c in range(PASSES)]
        above_zero = [grouped.tile([P, CH, PACK], BF16, tag="above_zero", name="above_zero%d" % c, align_bytes=64) for c in range(PASSES)]
        h_grouped = [grouped.tile([P, CH, PACK], BF16, tag="h_grouped", name="h_grouped%d" % c, align_bytes=64) for c in range(PASSES)]
        dz_grouped = [grouped.tile([P, CH, PACK], BF16, tag="dz_grouped", name="dz_grouped%d" % c, align_bytes=64) for c in range(PASSES)]

        def interleave_h(c):
            nc.scalar.copy(
                out=h_grouped[c][:].rearrange("p (b i) j -> p b j i", i=4),
                in_=h_raw[c][:].rearrange("p j (b i) -> p b j i", i=4),
            )

        def quantise_h(c):
            nc.vector.quantize_mx(
                out=h_codes[:, c, :].bitcast(E4M3_X4),
                scales=h_scales[:, c, :],
                in_=h_grouped[c][:].rearrange("p w j -> p (w j)"),
            )

        def mask(c, lo, width):
            nc.vector.scalar_tensor_tensor(
                out=dz_grouped[c][:, lo : lo + width, :],
                in0=z_raw[c][:, :, lo : lo + width].rearrange("p j w -> p w j"),
                scalar=0.0,
                in1=g_raw[c][:, :, lo : lo + width].rearrange("p j w -> p w j"),
                op0=ALU.is_gt,
                op1=ALU.mult,
            )

        def interleave_g(c, lo, width):
            cols = slice(lo, lo + width)
            nc.scalar.copy(
                out=g_grouped[c][:, cols, :].rearrange("p (b i) j -> p b j i", i=4),
                in_=g_raw[c][:, :, cols].rearrange("p j (b i) -> p b j i", i=4),
            )

        def compare(c, lo, width):
            cols = slice(lo, lo + width)
            nc.vector.tensor_scalar(
                out=above_zero[c][:, cols, :].rearrange("p (b i) j -> p b j i", i=4),
                in0=z_raw[c][:, :, cols].rearrange("p j (b i) -> p b j i", i=4),
                scalar1=0.0,
                scalar2=None,
                op0=ALU.is_gt,
            )

        def select(c, lo, width):
            cols = slice(lo, lo + width)
            nc.vector.tensor_tensor(
                out=dz_grouped[c][:, cols, :].rearrange("p w j -> p (w j)"),
                in0=above_zero[c][:, cols, :].rearrange("p w j -> p (w j)"),
                in1=g_grouped[c][:, cols, :].rearrange("p w j -> p (w j)"),
                op=ALU.mult,
            )

        def quantise_dz(c, lo, width):
            cols = slice(lo, lo + width)
            nc.vector.quantize_mx(
                out=dz_codes[:, c, cols].bitcast(E5M2_X4),
                scales=dz_scales[:, c, cols],
                in_=dz_grouped[c][:, cols, :].rearrange("p w j -> p (w j)"),
            )

        def multiply(c, lo, width):
            quantise_dz(c, lo, width)
            passes_of(c, lo, width)

        def passes_of(c, lo, width):
            for o in range(lo // P, (lo + width) // P):
                o_cols = slice(o * P, (o + 1) * P)
                nc.tensor.matmul_mx(
                    out=acc[o][:],
                    lhsT=dz_codes[:, c, o_cols].bitcast(E5M2_X4),
                    lhsT_scale=dz_scales[:, c, o_cols],
                    rhs=h_codes[:, c, :].bitcast(E4M3_X4),
                    rhs_scale=h_scales[:, c, :],
                    start=(c == 0),
                    stop=(c == LAST),
                )
                if c == LAST:
                    result = results.tile([P, CH], F32)
                    if o == O_TILES - 1:
                        for i_lo in (0, HALF):
                            i_cols = slice(i_lo, i_lo + HALF)
                            nc.vector.tensor_copy(out=result[:, i_cols], in_=acc[o][:, i_cols])
                            nc.sync.dma_start(out=out[o_cols, i_cols], in_=result[:, i_cols])
                    else:
                        nc.scalar.copy(out=result[:], in_=acc[o][:])
                        nc.sync.dma_start(out=out[o_cols, :], in_=result[:])

        for c in range(LAST):
            interleave_h(c)
            if c == 2:
                passes_of(1, 0, CH)
            if c >= 1:
                interleave_g(c, HALF, HALF)
                compare(c, HALF, HALF)
            quantise_h(c)
            mask(c, 0, HALF)
            if c >= 1:
                select(c, HALF, HALF)
            else:
                mask(c, HALF, HALF)
            if c == 1:
                quantise_dz(c, 0, HALF)
                quantise_dz(c, HALF, HALF)
            else:
                multiply(c, 0, HALF)
                multiply(c, HALF, HALF)
        interleave_h(LAST)
        mask(LAST, 0, P)
        mask(LAST, P, P)
        quantise_h(LAST)
        multiply(LAST, 0, HALF)
        mask(LAST, 2 * P, P)
        mask(LAST, 3 * P, P // 2)
        multiply(LAST, 2 * P, P)
        mask(LAST, 3 * P + P // 2, P // 2)
        quantise_dz(LAST, 3 * P, P // 2)
        multiply(LAST, 3 * P + P // 2, P // 2)
